import numpy as np
import ml_dtypes


def mxq(x, axis, fmt="e4m3"):
    dtype, down = {"e4m3": (ml_dtypes.float8_e4m3fn, 7), "e5m2": (ml_dtypes.float8_e5m2, 14)}[fmt]
    v = np.moveaxis(np.asarray(x, np.float32).astype(ml_dtypes.bfloat16).astype(np.float64), axis, -1)
    blocks = v.reshape(v.shape[:-1] + (-1, 32))
    amax = np.abs(blocks).max(-1, keepdims=True)
    byte = np.maximum(np.where(amax > 0, np.frexp(amax)[1] - 1 + 127, 0) - down, 1)
    scale = np.exp2(byte - 127.0)
    codes = (blocks / scale).astype(np.float32).astype(dtype).astype(np.float64)
    return np.moveaxis((codes * scale).reshape(v.shape), -1, axis)


WIDE = False


def mx_kscale(k):
    if not WIDE:
        return np.ones(k)
    levels = np.array([10, -10, 5, -5, 0])
    a = np.random.permutation(np.resize(levels, k // 512 * 4)).reshape(k // 512, 4)
    idx = np.arange(k)
    return np.exp2(a[idx // 512, idx % 128 // 32])


BF16 = ml_dtypes.bfloat16


def bf(x):
    return np.asarray(x, np.float32).astype(BF16)


def f64(x):
    return np.asarray(x).astype(np.float64)


E2M1 = np.array([0.0, 0.5, 1.0, 1.5, 2.0, 3.0, 4.0, 6.0, -0.0, -0.5, -1.0, -1.5, -2.0, -3.0, -4.0, -6.0])


def pack_weight(w, fmt):
    k, n = w.shape
    w = f64(bf(w)).reshape(k // 32, 32, n)
    amax = np.abs(w).max(1)
    if fmt == "e4m3":
        byte = np.frexp(amax)[1] - 1 + 127 - 7
    else:
        mant, ex = np.frexp(amax / 6.0)
        byte = np.where(mant > 0.5, ex, ex - 1) + 127
    byte = np.clip(np.where(amax > 0, byte, 1), 1, 254)
    scaled = (w * np.exp2(127.0 - byte)[:, None, :]).reshape(k, n).astype(np.float32)
    by_word = np.ascontiguousarray(scaled.reshape(k // 512, 128, 4, n).transpose(0, 1, 3, 2))
    if fmt == "e4m3":
        words = by_word.astype(ml_dtypes.float8_e4m3fn).view(np.uint8)
    else:
        c = by_word.astype(ml_dtypes.float4_e2m1fn).view(np.uint8) & 0xF
        words = c[..., 0::2] | (c[..., 1::2] << 4)
    return np.ascontiguousarray(words), np.ascontiguousarray(byte.astype(np.uint8).reshape(k // 512, 16, n))


def unpack_weight(words, scales, fmt):
    g, p, n, _ = words.shape
    if fmt == "e4m3":
        vals = np.ascontiguousarray(words).view(ml_dtypes.float8_e4m3fn).astype(np.float64)
    else:
        nib = np.empty((g, p, n, 4), np.uint8)
        nib[..., 0::2] = words & 0xF
        nib[..., 1::2] = words >> 4
        vals = E2M1[nib]
    vals = vals * np.repeat(np.exp2(scales.astype(np.float64) - 127.0), 8, axis=1)[..., None]
    return vals.transpose(0, 1, 3, 2).reshape(g * 512, n)


B, T, DX, DY, F = 128, 34, 1024, 512, 2
MIN_CONTEXT = 1
G = 1.5 / DY ** 0.25


def setup_inputs():
    s, t = mx_kscale(DX), mx_kscale(DY)
    embeddings = bf(np.random.standard_normal((B, T, DX)) * s)
    contexts = bf(np.random.standard_normal((B, T, DY)) * G / t)
    stack = (np.random.standard_normal((F, DY, DX)) * G / np.sqrt(DX) * t[:, None] / s).swapaxes(1, 2)
    words, scales = pack_weight(stack.reshape(-1, DY), "e4m3")
    return {"embeddings": embeddings,
            "contexts": contexts,
            "W_words": words,
            "W_scales": scales}


def reference(embeddings, contexts, W_words, W_scales):
    eq = mxq(f64(embeddings)[:, MIN_CONTEXT:T], 2, "e4m3")
    cq = mxq(f64(contexts)[:, MIN_CONTEXT - 1:T - 1], 2, "e4m3")
    wq = unpack_weight(W_words, W_scales, "e4m3").reshape(F, DX, DY)
    losses = []
    for step in range(F):
        S = T - step - MIN_CONTEXT
        xw = eq[:, step:] @ wq[step]
        scores = mxq(xw, 2, "e4m3").transpose(1, 0, 2) @ cq[:, :S].transpose(1, 2, 0)
        pos = np.diagonal(scores, axis1=1, axis2=2)
        m = scores.max(2, keepdims=True)
        lse = np.log(np.exp(scores - m).sum(2)) + m[:, :, 0] - np.log(B * S)
        losses.append((lse - pos).T.reshape(-1))
    return np.concatenate(losses)

@@ -1,0 +1,286 @@
+import math
+from contextlib import ExitStack
+
+import concourse.mybir as mybir
+from concourse.masks import make_identity
+
+F32 = mybir.dt.float32
+BF16 = mybir.dt.bfloat16
+I32 = mybir.dt.int32
+U32 = mybir.dt.uint32
+U8 = mybir.dt.uint8
+FP8X4 = mybir.dt.float8_e4m3fn_x4
+ALU = mybir.AluOpType
+ACT = mybir.ActivationFunctionType
+AXIS = mybir.AxisListType
+
+P = 128
+SEQS = 128
+TIMES = 33
+DX = 1024
+DY = 512
+STEPS = 2
+PACK = 4
+K_PASS = P * PACK
+X_PASSES = DX // K_PASS
+E_CHUNKS = DY // P
+WORD_HALVES = 2
+PAIR = 2
+ROUNDS = (TIMES + PAIR - 1) // PAIR
+TILES = STEPS * TIMES - 1
+
+FLOPS = 2 * TILES * SEQS * DX * DY + 2 * TILES * SEQS * SEQS * DY
+BYTES = SEQS * TIMES * (DX + DY) * 2 + STEPS * DX * DY + STEPS * DX * DY // 32 + TILES * SEQS * 4
+
+
+def times_of(r):
+    return list(range(PAIR * r, min(PAIR * r + PAIR, TIMES)))
+
+
+def pair_tiles_of(r):
+    return [(s, step) for s in times_of(r) for step in range(STEPS) if s + step < TIMES]
+
+
+def tile_infonceloss_pa_t_e_kernel(tc, embeddings, contexts, W_words, W_scales, out):
+    nc = tc.nc
+    with ExitStack() as ctx:
+        consts = ctx.enter_context(tc.tile_pool(name="consts", bufs=1))
+        inputs = ctx.enter_context(tc.tile_pool(name="inputs", bufs=1))
+        grouped = ctx.enter_context(tc.tile_pool(name="grouped", bufs=2))
+        x_mx = ctx.enter_context(tc.tile_pool(name="x_mx", bufs=3))
+        c_mx = ctx.enter_context(tc.tile_pool(name="c_mx", bufs=4))
+        xw_mx = ctx.enter_context(tc.tile_pool(name="xw_mx", bufs=2))
+        work = ctx.enter_context(tc.tile_pool(name="work", bufs=2))
+        xt_banks = ctx.enter_context(tc.psum_pool(name="xt_banks", bufs=PAIR))
+        ct_banks = ctx.enter_context(tc.psum_pool(name="ct_banks", bufs=1))
+        xw_banks = ctx.enter_context(tc.psum_pool(name="xw_banks", bufs=PAIR * STEPS))
+        score_banks = ctx.enter_context(tc.psum_pool(name="score_banks", bufs=1))
+        ctx.enter_context(tc.manual_schedule())
+
+        ident_f32 = consts.tile([P, P], F32)
+        make_identity(nc, ident_f32[:])
+        ident_bf16 = consts.tile([P, P], BF16)
+        make_identity(nc, ident_bf16[:])
+
+        w_codes = consts.tile([P, STEPS * X_PASSES, DY], U32, align_bytes=64)
+        w_scales = consts.tile([P, STEPS * X_PASSES, DY], U8, align_bytes=64)
+        nc.vector.memset(w_scales[:].bitcast(I32), 0)
+
+        x_sb = {}
+        c_sb = {}
+
+        def load_x(r):
+            n = len(times_of(r))
+            x_rows = inputs.tile([P, n, DX], BF16, name="x_rows%d" % r)
+            nc.sync.dma_start(out=x_rows[:], in_=embeddings[:, 1 + PAIR * r : 1 + PAIR * r + n, :])
+            x_sb[r] = x_rows
+
+        def load_c(r):
+            n = len(times_of(r))
+            c_rows = inputs.tile([P, n, DY], BF16, name="c_rows%d" % r)
+            nc.sync.dma_start(out=c_rows[:], in_=contexts[:, PAIR * r : PAIR * r + n, :])
+            c_sb[r] = c_rows
+
+        load_x(0)
+        load_x(1)
+        scale_words = W_scales.bitcast(I32)
+        for quadrant in range(4):
+            nc.sync.dma_start(
+                out=w_scales[32 * quadrant : 32 * quadrant + 4].bitcast(I32),
+                in_=scale_words[:, 4 * quadrant : 4 * quadrant + 4, :].rearrange("g q n -> q g n"),
+            )
+        code_words = W_words.rearrange("g p n t -> g p (n t)").bitcast(I32)
+        for step in range(STEPS):
+            passes = slice(X_PASSES * step, X_PASSES * (step + 1))
+            nc.sync.dma_start(
+                out=w_codes[:, passes, :].bitcast(I32),
+                in_=code_words[passes].rearrange("g p n -> p g n"),
+            )
+        load_c(0)
+        load_c(1)
+        for r in range(2, ROUNDS):
+            load_x(r)
+            load_c(r)
+
+        neg_max = consts.tile([P, TILES], F32)
+        sum_exp = consts.tile([P, TILES], F32)
+        diagonal = consts.tile([P, TILES], F32)
+
+        x_codes, x_scales = {}, {}
+        c_codes, c_scales = {}, {}
+        xw_values = {}
+        xw_codes, xw_scales = {}, {}
+        scores = {}
+        on_diagonal = {}
+
+        def transpose_inputs(r):
+            n = len(times_of(r))
+            x_words = x_sb[r][:].bitcast(F32)
+            x_banks = []
+            for k in range(n):
+                xt = xt_banks.tile([P, X_PASSES, WORD_HALVES, SEQS], F32)
+                for g in range(X_PASSES):
+                    for u in range(WORD_HALVES):
+                        first = g * K_PASS // 2 + u
+                        nc.tensor.transpose(
+                            xt[:, g, u, :],
+                            x_words[:, k, first : (g + 1) * K_PASS // 2 : WORD_HALVES],
+                            ident_f32[:],
+                        )
+                x_banks.append(xt)
+            ct = ct_banks.tile([P, PAIR, E_CHUNKS, SEQS], BF16)
+            for k in range(n):
+                for t in range(E_CHUNKS):
+                    nc.tensor.transpose(ct[:, k, t, :], c_sb[r][:, k, t * P : (t + 1) * P], ident_bf16[:])
+
+            x_grouped = grouped.tile([P, PAIR, X_PASSES, SEQS, PACK], BF16, align_bytes=64)
+            for k in range(n):
+                nc.vector.tensor_copy(
+                    out=x_grouped[:].bitcast(F32)[:, k],
+                    in_=x_banks[k][:].rearrange("p g u b -> p g b u"),
+                )
+            c_grouped = grouped.tile([P, PAIR, SEQS, PACK], BF16, align_bytes=64)
+            nc.scalar.copy(out=c_grouped[:, :n], in_=ct[:, :n].rearrange("p k t j -> p k j t"))
+            return x_grouped, c_grouped
+
+        def quantise_inputs(r, x_grouped, c_grouped):
+            n = len(times_of(r))
+            xq = x_mx.tile([P, PAIR, X_PASSES, SEQS], U32, align_bytes=64)
+            xs = x_mx.tile([P, PAIR, X_PASSES, SEQS], U8, align_bytes=64)
+            nc.vector.quantize_mx(
+                out=xq[:, :n].rearrange("p k g b -> p (k g b)").bitcast(FP8X4),
+                scales=xs[:, :n].rearrange("p k g b -> p (k g b)"),
+                in_=x_grouped[:, :n].rearrange("p k g b t -> p (k g b t)"),
+            )
+            x_codes[r], x_scales[r] = xq, xs
+            cq = c_mx.tile([P, PAIR, SEQS], U32, align_bytes=64)
+            cs = c_mx.tile([P, PAIR, SEQS], U8, align_bytes=64)
+            nc.vector.quantize_mx(
+                out=cq[:, :n].rearrange("p k j -> p (k j)").bitcast(FP8X4),
+                scales=cs[:, :n].rearrange("p k j -> p (k j)"),
+                in_=c_grouped[:, :n].rearrange("p k j t -> p (k j t)"),
+            )
+            c_codes[r], c_scales[r] = cq, cs
+
+        def first_contraction(r):
+            xw_grouped = grouped.tile([P, PAIR * STEPS, SEQS, PACK], BF16, align_bytes=64)
+            for m, (s, step) in enumerate(pair_tiles_of(r)):
+                i = s + step
+                xw_bank = xw_banks.tile([P, E_CHUNKS, SEQS], F32)
+                for t in range(E_CHUNKS):
+                    e_cols = slice(t * P, (t + 1) * P)
+                    for g in range(X_PASSES):
+                        nc.tensor.matmul_mx(
+                            out=xw_bank[:, t, :],
+                            lhsT=w_codes[:, X_PASSES * step + g, e_cols].bitcast(FP8X4),
+                            lhsT_scale=w_scales[:, X_PASSES * step + g, e_cols],
+                            rhs=x_codes[i // PAIR][:, i % PAIR, g, :].bitcast(FP8X4),
+                            rhs_scale=x_scales[i // PAIR][:, i % PAIR, g, :],
+                            start=(g == 0),
+                            stop=(g == X_PASSES - 1),
+                        )
+                nc.scalar.copy(out=xw_grouped[:, m], in_=xw_bank[:].rearrange("p t b -> p b t"))
+            xw_values[r] = xw_grouped
+
+        def quantise_xw(r):
+            n = len(pair_tiles_of(r))
+            wq = xw_mx.tile([P, PAIR * STEPS, SEQS], U32, align_bytes=64)
+            ws = xw_mx.tile([P, PAIR * STEPS, SEQS], U8, align_bytes=64)
+            nc.vector.quantize_mx(
+                out=wq[:, :n].rearrange("p m b -> p (m b)").bitcast(FP8X4),
+                scales=ws[:, :n].rearrange("p m b -> p (m b)"),
+                in_=xw_values[r][:, :n].rearrange("p m b t -> p (m b t)"),
+            )
+            xw_codes[r], xw_scales[r] = wq, ws
+
+        def second_contraction(r):
+            score_bank = score_banks.tile([P, PAIR * STEPS, SEQS], F32)
+            for m, (s, step) in enumerate(pair_tiles_of(r)):
+                nc.tensor.matmul_mx(
+                    out=score_bank[:, m, :],
+                    lhsT=xw_codes[r][:, m, :].bitcast(FP8X4),
+                    lhsT_scale=xw_scales[r][:, m, :],
+                    rhs=c_codes[r][:, s % PAIR, :].bitcast(FP8X4),
+                    rhs_scale=c_scales[r][:, s % PAIR, :],
+                    start=True,
+                    stop=True,
+                )
+            scores[r] = score_bank
+
+        def first_column(r):
+            return PAIR * STEPS * r
+
+        def columns_of(r):
+            return slice(first_column(r), first_column(r) + len(pair_tiles_of(r)))
+
+        def mask_and_maximum(r):
+            n = len(pair_tiles_of(r))
+            masked = work.tile([P, PAIR * STEPS, SEQS], F32)
+            nc.vector.tensor_tensor(
+                out=masked[:, :n],
+                in0=scores[r][:, :n],
+                in1=ident_f32[:].unsqueeze(1).to_broadcast([P, n, SEQS]),
+                op=ALU.mult,
+            )
+            on_diagonal[r] = masked
+            nc.vector.tensor_reduce(
+                out=neg_max[:, columns_of(r)], in_=scores[r][:, :n], axis=AXIS.X, op=ALU.max, negate=True
+            )
+
+        def exponentials(r):
+            for m in range(len(pair_tiles_of(r))):
+                column = slice(first_column(r) + m, first_column(r) + m + 1)
+                exp_values = work.tile([P, SEQS], F32)
+                nc.scalar.activation(
+                    out=exp_values[:],
+                    in_=scores[r][:, m, :],
+                    func=ACT.Exp,
+                    bias=neg_max[:, column],
+                    scale=1.0,
+                    accum_out=sum_exp[:, column],
+                )
+
+        def sum_diagonal(r):
+            n = len(pair_tiles_of(r))
+            nc.vector.tensor_reduce(
+                out=diagonal[:, columns_of(r)], in_=on_diagonal[r][:, :n], axis=AXIS.X, op=ALU.add
+            )
+
+        def live(r):
+            return 0 <= r < ROUNDS
+
+        for turn in range(ROUNDS + 4):
+            if live(turn - 4):
+                mask_and_maximum(turn - 4)
+                exponentials(turn - 4)
+            if live(turn - 3):
+                quantise_xw(turn - 3)
+            if live(turn):
+                x_grouped, c_grouped = transpose_inputs(turn)
+            if live(turn - 4):
+                sum_diagonal(turn - 4)
+            if live(turn):
+                quantise_inputs(turn, x_grouped, c_grouped)
+            if live(turn - 2):
+                first_contraction(turn - 2)
+            if live(turn - 3):
+                second_contraction(turn - 3)
+
+        shift = consts.tile([P, TILES], F32)
+        nc.vector.tensor_tensor(out=shift[:], in0=neg_max[:], in1=diagonal[:], op=ALU.add)
+        log_sum = consts.tile([P, TILES], F32)
+        nc.scalar.activation(out=log_sum[:], in_=sum_exp[:], func=ACT.Ln)
+        centred = consts.tile([P, TILES], F32)
+        nc.vector.tensor_tensor(out=centred[:], in0=log_sum[:], in1=shift[:], op=ALU.subtract)
+        first_row = 0
+        for step in range(STEPS):
+            n_times = TIMES - step
+            loss = consts.tile([P, n_times], F32, name="loss%d" % step)
+            nc.vector.tensor_scalar_add(
+                out=loss[:], in0=centred[:, step:TILES:STEPS], scalar1=-math.log(SEQS * n_times)
+            )
+            nc.sync.dma_start(
+                out=out[first_row : first_row + SEQS * n_times].rearrange("(b s) -> b s", s=n_times),
+                in_=loss[:],
+            )
+            first_row += SEQS * n_times

@@ -38,7 +38,11 @@ def times_of(r):
 
 
 def pair_tiles_of(r):
-    return [(s, step) for s in times_of(r) for step in range(STEPS) if s + step < TIMES]
+    return [(i - step, step) for i in times_of(r) for step in reversed(range(STEPS)) if i - step >= 0]
+
+
+def column_of(s, step):
+    return STEPS * s + step
 
 
 def tile_infonceloss_pa_t_e_kernel(tc, embeddings, contexts, W_words, W_scales, out):
@@ -47,8 +51,8 @@ def tile_infonceloss_pa_t_e_kernel(tc, embeddings, contexts, W_words, W_scales, 
         consts = ctx.enter_context(tc.tile_pool(name="consts", bufs=1))
         inputs = ctx.enter_context(tc.tile_pool(name="inputs", bufs=1))
         grouped = ctx.enter_context(tc.tile_pool(name="grouped", bufs=2))
-        x_mx = ctx.enter_context(tc.tile_pool(name="x_mx", bufs=3))
-        c_mx = ctx.enter_context(tc.tile_pool(name="c_mx", bufs=4))
+        x_mx = ctx.enter_context(tc.tile_pool(name="x_mx", bufs=2))
+        c_mx = ctx.enter_context(tc.tile_pool(name="c_mx", bufs=3))
         xw_mx = ctx.enter_context(tc.tile_pool(name="xw_mx", bufs=2))
         work = ctx.enter_context(tc.tile_pool(name="work", bufs=2))
         xt_banks = ctx.enter_context(tc.psum_pool(name="xt_banks", bufs=PAIR))
@@ -65,6 +69,11 @@ def tile_infonceloss_pa_t_e_kernel(tc, embeddings, contexts, W_words, W_scales, 
         w_codes = consts.tile([P, STEPS * X_PASSES, DY], U32, align_bytes=64)
         w_scales = consts.tile([P, STEPS * X_PASSES, DY], U8, align_bytes=64)
         nc.vector.memset(w_scales[:].bitcast(I32), 0)
+
+        zero = consts.tile([P, 1], F32)
+        nc.vector.memset(zero[:], 0.0)
+        one = consts.tile([P, 1], F32)
+        nc.scalar.activation(out=one[:], in_=zero[:], func=ACT.Exp)
 
         x_sb = {}
         c_sb = {}
@@ -83,6 +92,7 @@ def tile_infonceloss_pa_t_e_kernel(tc, embeddings, contexts, W_words, W_scales, 
 
         load_x(0)
         load_x(1)
+        load_c(0)
         scale_words = W_scales.bitcast(I32)
         for quadrant in range(4):
             nc.sync.dma_start(
@@ -96,11 +106,10 @@ def tile_infonceloss_pa_t_e_kernel(tc, embeddings, contexts, W_words, W_scales, 
                 out=w_codes[:, passes, :].bitcast(I32),
                 in_=code_words[passes].rearrange("g p n -> p g n"),
             )
-        load_c(0)
-        load_c(1)
         for r in range(2, ROUNDS):
             load_x(r)
-            load_c(r)
+            load_c(r - 1)
+        load_c(ROUNDS - 1)
 
         neg_max = consts.tile([P, TILES], F32)
         sum_exp = consts.tile([P, TILES], F32)
@@ -108,16 +117,14 @@ def tile_infonceloss_pa_t_e_kernel(tc, embeddings, contexts, W_words, W_scales, 
 
         x_codes, x_scales = {}, {}
         c_codes, c_scales = {}, {}
-        xw_values = {}
+        x_values, c_values, xw_values = {}, {}, {}
         xw_codes, xw_scales = {}, {}
         scores = {}
-        on_diagonal = {}
 
-        def transpose_inputs(r):
-            n = len(times_of(r))
+        def transpose_x(r):
             x_words = x_sb[r][:].bitcast(F32)
-            x_banks = []
-            for k in range(n):
+            x_grouped = grouped.tile([P, PAIR, X_PASSES, SEQS, PACK], BF16, align_bytes=64)
+            for k in range(len(times_of(r))):
                 xt = xt_banks.tile([P, X_PASSES, WORD_HALVES, SEQS], F32)
                 for g in range(X_PASSES):
                     for u in range(WORD_HALVES):
@@ -127,38 +134,40 @@ def tile_infonceloss_pa_t_e_kernel(tc, embeddings, contexts, W_words, W_scales, 
                             x_words[:, k, first : (g + 1) * K_PASS // 2 : WORD_HALVES],
                             ident_f32[:],
                         )
-                x_banks.append(xt)
+                nc.vector.tensor_copy(
+                    out=x_grouped[:].bitcast(F32)[:, k], in_=xt[:].rearrange("p g u b -> p g b u")
+                )
+            x_values[r] = x_grouped
+
+        def transpose_c(r):
+            n = len(times_of(r))
             ct = ct_banks.tile([P, PAIR, E_CHUNKS, SEQS], BF16)
             for k in range(n):
                 for t in range(E_CHUNKS):
                     nc.tensor.transpose(ct[:, k, t, :], c_sb[r][:, k, t * P : (t + 1) * P], ident_bf16[:])
-
-            x_grouped = grouped.tile([P, PAIR, X_PASSES, SEQS, PACK], BF16, align_bytes=64)
-            for k in range(n):
-                nc.vector.tensor_copy(
-                    out=x_grouped[:].bitcast(F32)[:, k],
-                    in_=x_banks[k][:].rearrange("p g u b -> p g b u"),
-                )
             c_grouped = grouped.tile([P, PAIR, SEQS, PACK], BF16, align_bytes=64)
             nc.scalar.copy(out=c_grouped[:, :n], in_=ct[:, :n].rearrange("p k t j -> p k j t"))
-            return x_grouped, c_grouped
+            c_values[r] = c_grouped
 
-        def quantise_inputs(r, x_grouped, c_grouped):
+        def quantise_x(r):
             n = len(times_of(r))
             xq = x_mx.tile([P, PAIR, X_PASSES, SEQS], U32, align_bytes=64)
             xs = x_mx.tile([P, PAIR, X_PASSES, SEQS], U8, align_bytes=64)
             nc.vector.quantize_mx(
                 out=xq[:, :n].rearrange("p k g b -> p (k g b)").bitcast(FP8X4),
                 scales=xs[:, :n].rearrange("p k g b -> p (k g b)"),
-                in_=x_grouped[:, :n].rearrange("p k g b t -> p (k g b t)"),
+                in_=x_values[r][:, :n].rearrange("p k g b t -> p (k g b t)"),
             )
             x_codes[r], x_scales[r] = xq, xs
+
+        def quantise_c(r):
+            n = len(times_of(r))
             cq = c_mx.tile([P, PAIR, SEQS], U32, align_bytes=64)
             cs = c_mx.tile([P, PAIR, SEQS], U8, align_bytes=64)
             nc.vector.quantize_mx(
                 out=cq[:, :n].rearrange("p k j -> p (k j)").bitcast(FP8X4),
                 scales=cs[:, :n].rearrange("p k j -> p (k j)"),
-                in_=c_grouped[:, :n].rearrange("p k j t -> p (k j t)"),
+                in_=c_values[r][:, :n].rearrange("p k j t -> p (k j t)"),
             )
             c_codes[r], c_scales[r] = cq, cs
 
@@ -183,14 +192,17 @@ def tile_infonceloss_pa_t_e_kernel(tc, embeddings, contexts, W_words, W_scales, 
             xw_values[r] = xw_grouped
 
         def quantise_xw(r):
-            n = len(pair_tiles_of(r))
             wq = xw_mx.tile([P, PAIR * STEPS, SEQS], U32, align_bytes=64)
             ws = xw_mx.tile([P, PAIR * STEPS, SEQS], U8, align_bytes=64)
-            nc.vector.quantize_mx(
-                out=wq[:, :n].rearrange("p m b -> p (m b)").bitcast(FP8X4),
-                scales=ws[:, :n].rearrange("p m b -> p (m b)"),
-                in_=xw_values[r][:, :n].rearrange("p m b t -> p (m b t)"),
-            )
+            tiles = pair_tiles_of(r)
+            for i in times_of(r):
+                mine = [m for m, (s, step) in enumerate(tiles) if s + step == i]
+                slots = slice(mine[0], mine[-1] + 1)
+                nc.vector.quantize_mx(
+                    out=wq[:, slots].rearrange("p m b -> p (m b)").bitcast(FP8X4),
+                    scales=ws[:, slots].rearrange("p m b -> p (m b)"),
+                    in_=xw_values[r][:, slots].rearrange("p m b t -> p (m b t)"),
+                )
             xw_codes[r], xw_scales[r] = wq, ws
 
         def second_contraction(r):
@@ -200,35 +212,39 @@ def tile_infonceloss_pa_t_e_kernel(tc, embeddings, contexts, W_words, W_scales, 
                     out=score_bank[:, m, :],
                     lhsT=xw_codes[r][:, m, :].bitcast(FP8X4),
                     lhsT_scale=xw_scales[r][:, m, :],
-                    rhs=c_codes[r][:, s % PAIR, :].bitcast(FP8X4),
-                    rhs_scale=c_scales[r][:, s % PAIR, :],
+                    rhs=c_codes[s // PAIR][:, s % PAIR, :].bitcast(FP8X4),
+                    rhs_scale=c_scales[s // PAIR][:, s % PAIR, :],
                     start=True,
                     stop=True,
                 )
             scores[r] = score_bank
 
         def first_column(r):
-            return PAIR * STEPS * r
+            s, step = pair_tiles_of(r)[0]
+            return column_of(s, step)
 
-        def columns_of(r):
-            return slice(first_column(r), first_column(r) + len(pair_tiles_of(r)))
-
-        def mask_and_maximum(r):
+        def statistics(r):
             n = len(pair_tiles_of(r))
-            masked = work.tile([P, PAIR * STEPS, SEQS], F32)
-            nc.vector.tensor_tensor(
-                out=masked[:, :n],
-                in0=scores[r][:, :n],
-                in1=ident_f32[:].unsqueeze(1).to_broadcast([P, n, SEQS]),
-                op=ALU.mult,
-            )
-            on_diagonal[r] = masked
+            for m in range(n):
+                column = slice(first_column(r) + m, first_column(r) + m + 1)
+                on_diagonal = work.tile([P, SEQS], F32)
+                nc.vector.scalar_tensor_tensor(
+                    out=on_diagonal[:],
+                    in0=scores[r][:, m, :],
+                    scalar=1.0,
+                    in1=ident_f32[:],
+                    op0=ALU.mult,
+                    op1=ALU.mult,
+                    accum_out=diagonal[:, column],
+                )
             nc.vector.tensor_reduce(
-                out=neg_max[:, columns_of(r)], in_=scores[r][:, :n], axis=AXIS.X, op=ALU.max, negate=True
+                out=neg_max[:, first_column(r) : first_column(r) + n],
+                in_=scores[r][:, :n],
+                axis=AXIS.X,
+                op=ALU.max,
+                negate=True,
             )
-
-        def exponentials(r):
-            for m in range(len(pair_tiles_of(r))):
+            for m in range(n):
                 column = slice(first_column(r) + m, first_column(r) + m + 1)
                 exp_values = work.tile([P, SEQS], F32)
                 nc.scalar.activation(
@@ -240,31 +256,25 @@ def tile_infonceloss_pa_t_e_kernel(tc, embeddings, contexts, W_words, W_scales, 
                     accum_out=sum_exp[:, column],
                 )
 
-        def sum_diagonal(r):
-            n = len(pair_tiles_of(r))
-            nc.vector.tensor_reduce(
-                out=diagonal[:, columns_of(r)], in_=on_diagonal[r][:, :n], axis=AXIS.X, op=ALU.add
-            )
-
         def live(r):
             return 0 <= r < ROUNDS
 
-        for turn in range(ROUNDS + 4):
-            if live(turn - 4):
-                mask_and_maximum(turn - 4)
-                exponentials(turn - 4)
-            if live(turn - 3):
-                quantise_xw(turn - 3)
-            if live(turn):
-                x_grouped, c_grouped = transpose_inputs(turn)
-            if live(turn - 4):
-                sum_diagonal(turn - 4)
-            if live(turn):
-                quantise_inputs(turn, x_grouped, c_grouped)
+        for turn in range(ROUNDS + 3):
+            if live(turn - 1):
+                quantise_x(turn - 1)
             if live(turn - 2):
-                first_contraction(turn - 2)
+                quantise_c(turn - 2)
             if live(turn - 3):
-                second_contraction(turn - 3)
+                statistics(turn - 3)
+            if live(turn - 2):
+                quantise_xw(turn - 2)
+            if live(turn):
+                transpose_x(turn)
+            if live(turn - 1):
+                transpose_c(turn - 1)
+                first_contraction(turn - 1)
+            if live(turn - 2):
+                second_contraction(turn - 2)
 
         shift = consts.tile([P, TILES], F32)
         nc.vector.tensor_tensor(out=shift[:], in0=neg_max[:], in1=diagonal[:], op=ALU.add)

@@ -55,6 +55,7 @@ def tile_infonceloss_pa_t_e_kernel(tc, embeddings, contexts, W_words, W_scales, 
         c_mx = ctx.enter_context(tc.tile_pool(name="c_mx", bufs=3))
         xw_mx = ctx.enter_context(tc.tile_pool(name="xw_mx", bufs=2))
         work = ctx.enter_context(tc.tile_pool(name="work", bufs=2))
+        paired = ctx.enter_context(tc.tile_pool(name="paired", bufs=2))
         xt_banks = ctx.enter_context(tc.psum_pool(name="xt_banks", bufs=PAIR))
         ct_banks = ctx.enter_context(tc.psum_pool(name="ct_banks", bufs=1))
         xw_banks = ctx.enter_context(tc.psum_pool(name="xw_banks", bufs=PAIR * STEPS))
@@ -63,8 +64,6 @@ def tile_infonceloss_pa_t_e_kernel(tc, embeddings, contexts, W_words, W_scales, 
 
         ident_f32 = consts.tile([P, P], F32)
         make_identity(nc, ident_f32[:])
-        ident_bf16 = consts.tile([P, P], BF16)
-        make_identity(nc, ident_bf16[:])
 
         w_codes = consts.tile([P, STEPS * X_PASSES, DY], U32, align_bytes=64)
         w_scales = consts.tile([P, STEPS * X_PASSES, DY], U8, align_bytes=64)
@@ -120,6 +119,7 @@ def tile_infonceloss_pa_t_e_kernel(tc, embeddings, contexts, W_words, W_scales, 
         x_values, c_values, xw_values = {}, {}, {}
         xw_codes, xw_scales = {}, {}
         scores = {}
+        c_pairs = {}
 
         def transpose_x(r):
             x_words = x_sb[r][:].bitcast(F32)
@@ -139,14 +139,28 @@ def tile_infonceloss_pa_t_e_kernel(tc, embeddings, contexts, W_words, W_scales, 
                 )
             x_values[r] = x_grouped
 
+        def pair_up_c(r):
+            n = len(times_of(r))
+            c_paired = paired.tile([P, PAIR, WORD_HALVES, P, 2], BF16)
+            nc.gpsimd.tensor_scalar(
+                out=c_paired[:, :n].rearrange("j k u p h -> j (k u) p h"),
+                in0=c_sb[r][:, :n].rearrange("j k (u h p) -> j (k u) p h", u=WORD_HALVES, h=2),
+                scalar1=1.0,
+                scalar2=0.0,
+                op0=ALU.mult,
+                op1=ALU.add,
+            )
+            c_pairs[r] = c_paired
+
         def transpose_c(r):
             n = len(times_of(r))
-            ct = ct_banks.tile([P, PAIR, E_CHUNKS, SEQS], BF16)
+            c_words = c_pairs[r][:].bitcast(F32)
+            ct = ct_banks.tile([P, PAIR, WORD_HALVES, SEQS], F32)
             for k in range(n):
-                for t in range(E_CHUNKS):
-                    nc.tensor.transpose(ct[:, k, t, :], c_sb[r][:, k, t * P : (t + 1) * P], ident_bf16[:])
+                for u in range(WORD_HALVES):
+                    nc.tensor.transpose(ct[:, k, u, :], c_words[:, k, u, :, 0], ident_f32[:])
             c_grouped = grouped.tile([P, PAIR, SEQS, PACK], BF16, align_bytes=64)
-            nc.scalar.copy(out=c_grouped[:, :n], in_=ct[:, :n].rearrange("p k t j -> p k j t"))
+            nc.scalar.copy(out=c_grouped[:].bitcast(F32)[:, :n], in_=ct[:, :n].rearrange("p k u j -> p k j u"))
             c_values[r] = c_grouped
 
         def quantise_x(r):
@@ -260,6 +274,8 @@ def tile_infonceloss_pa_t_e_kernel(tc, embeddings, contexts, W_words, W_scales, 
             return 0 <= r < ROUNDS
 
         for turn in range(ROUNDS + 3):
+            if live(turn):
+                pair_up_c(turn)
             if live(turn - 1):
                 quantise_x(turn - 1)
             if live(turn - 2):

@@ -55,7 +55,7 @@ def tile_infonceloss_pa_t_e_kernel(tc, embeddings, contexts, W_words, W_scales, 
         c_mx = ctx.enter_context(tc.tile_pool(name="c_mx", bufs=3))
         xw_mx = ctx.enter_context(tc.tile_pool(name="xw_mx", bufs=2))
         work = ctx.enter_context(tc.tile_pool(name="work", bufs=2))
-        paired = ctx.enter_context(tc.tile_pool(name="paired", bufs=2))
+        paired = ctx.enter_context(tc.tile_pool(name="paired", bufs=1))
         xt_banks = ctx.enter_context(tc.psum_pool(name="xt_banks", bufs=PAIR))
         ct_banks = ctx.enter_context(tc.psum_pool(name="ct_banks", bufs=1))
         xw_banks = ctx.enter_context(tc.psum_pool(name="xw_banks", bufs=PAIR * STEPS))
@@ -274,20 +274,20 @@ def tile_infonceloss_pa_t_e_kernel(tc, embeddings, contexts, W_words, W_scales, 
             return 0 <= r < ROUNDS
 
         for turn in range(ROUNDS + 3):
-            if live(turn):
-                pair_up_c(turn)
-            if live(turn - 1):
-                quantise_x(turn - 1)
             if live(turn - 2):
-                quantise_c(turn - 2)
+                transpose_c(turn - 2)
             if live(turn - 3):
                 statistics(turn - 3)
-            if live(turn - 2):
-                quantise_xw(turn - 2)
+            if live(turn - 1):
+                pair_up_c(turn - 1)
             if live(turn):
                 transpose_x(turn)
+            if live(turn - 2):
+                quantise_c(turn - 2)
+                quantise_xw(turn - 2)
+            if live(turn):
+                quantise_x(turn)
             if live(turn - 1):
-                transpose_c(turn - 1)
                 first_contraction(turn - 1)
             if live(turn - 2):
                 second_contraction(turn - 2)

@@ -23,6 +23,7 @@ STEPS = 2
 PACK = 4
 K_PASS = P * PACK
 X_PASSES = DX // K_PASS
+W_PASSES = STEPS * X_PASSES
 E_CHUNKS = DY // P
 WORD_HALVES = 2
 PAIR = 2
@@ -55,7 +56,6 @@ def tile_infonceloss_pa_t_e_kernel(tc, embeddings, contexts, W_words, W_scales, 
         c_mx = ctx.enter_context(tc.tile_pool(name="c_mx", bufs=3))
         xw_mx = ctx.enter_context(tc.tile_pool(name="xw_mx", bufs=2))
         work = ctx.enter_context(tc.tile_pool(name="work", bufs=2))
-        paired = ctx.enter_context(tc.tile_pool(name="paired", bufs=1))
         xt_banks = ctx.enter_context(tc.psum_pool(name="xt_banks", bufs=PAIR))
         ct_banks = ctx.enter_context(tc.psum_pool(name="ct_banks", bufs=1))
         xw_banks = ctx.enter_context(tc.psum_pool(name="xw_banks", bufs=PAIR * STEPS))
@@ -65,9 +65,11 @@ def tile_infonceloss_pa_t_e_kernel(tc, embeddings, contexts, W_words, W_scales, 
         ident_f32 = consts.tile([P, P], F32)
         make_identity(nc, ident_f32[:])
 
-        w_codes = consts.tile([P, STEPS * X_PASSES, DY], U32, align_bytes=64)
-        w_scales = consts.tile([P, STEPS * X_PASSES, DY], U8, align_bytes=64)
-        nc.vector.memset(w_scales[:].bitcast(I32), 0)
+        w_loaded = consts.tile([P, W_PASSES, DY], I32)
+        w_codes = consts.tile([P, W_PASSES, DY], I32, align_bytes=64)
+        w_scales_loaded = consts.tile([P, DY], U8)
+        w_scales = consts.tile([P, DY], U8, align_bytes=64)
+        nc.vector.memset(w_scales_loaded[:].bitcast(I32), 0)
 
         zero = consts.tile([P, 1], F32)
         nc.vector.memset(zero[:], 0.0)
@@ -95,20 +97,31 @@ def tile_infonceloss_pa_t_e_kernel(tc, embeddings, contexts, W_words, W_scales, 
         scale_words = W_scales.bitcast(I32)
         for quadrant in range(4):
             nc.sync.dma_start(
-                out=w_scales[32 * quadrant : 32 * quadrant + 4].bitcast(I32),
-                in_=scale_words[:, 4 * quadrant : 4 * quadrant + 4, :].rearrange("g q n -> q g n"),
+                out=w_scales_loaded[32 * quadrant : 32 * quadrant + 4 * W_PASSES].bitcast(I32),
+                in_=scale_words[:, 4 * quadrant : 4 * quadrant + 4, :],
             )
         code_words = W_words.rearrange("g p n t -> g p (n t)").bitcast(I32)
         for step in range(STEPS):
             passes = slice(X_PASSES * step, X_PASSES * (step + 1))
             nc.sync.dma_start(
-                out=w_codes[:, passes, :].bitcast(I32),
+                out=w_loaded[:, passes, :],
                 in_=code_words[passes].rearrange("g p n -> p g n"),
             )
         for r in range(2, ROUNDS):
             load_x(r)
             load_c(r - 1)
         load_c(ROUNDS - 1)
+
+        def permute_w():
+            nc.vector.tensor_copy(
+                out=w_scales[:].rearrange("p (u h m) -> p u m h", u=WORD_HALVES, h=2),
+                in_=w_scales_loaded[:].rearrange("p (u m h) -> p u m h", u=WORD_HALVES, h=2),
+            )
+            for g in range(W_PASSES):
+                nc.vector.tensor_copy(
+                    out=w_codes[:, g, :].rearrange("p (u h m) -> p u h m", u=WORD_HALVES, h=2),
+                    in_=w_loaded[:, g, :].rearrange("p (u m h) -> p u h m", u=WORD_HALVES, h=2),
+                )
 
         neg_max = consts.tile([P, TILES], F32)
         sum_exp = consts.tile([P, TILES], F32)
@@ -119,7 +132,6 @@ def tile_infonceloss_pa_t_e_kernel(tc, embeddings, contexts, W_words, W_scales, 
         x_values, c_values, xw_values = {}, {}, {}
         xw_codes, xw_scales = {}, {}
         scores = {}
-        c_pairs = {}
 
         def transpose_x(r):
             x_words = x_sb[r][:].bitcast(F32)
@@ -139,26 +151,13 @@ def tile_infonceloss_pa_t_e_kernel(tc, embeddings, contexts, W_words, W_scales, 
                 )
             x_values[r] = x_grouped
 
-        def pair_up_c(r):
-            n = len(times_of(r))
-            c_paired = paired.tile([P, PAIR, WORD_HALVES, P, 2], BF16)
-            nc.gpsimd.tensor_scalar(
-                out=c_paired[:, :n].rearrange("j k u p h -> j (k u) p h"),
-                in0=c_sb[r][:, :n].rearrange("j k (u h p) -> j (k u) p h", u=WORD_HALVES, h=2),
-                scalar1=1.0,
-                scalar2=0.0,
-                op0=ALU.mult,
-                op1=ALU.add,
-            )
-            c_pairs[r] = c_paired
-
         def transpose_c(r):
             n = len(times_of(r))
-            c_words = c_pairs[r][:].bitcast(F32)
+            c_words = c_sb[r][:].bitcast(F32)
             ct = ct_banks.tile([P, PAIR, WORD_HALVES, SEQS], F32)
             for k in range(n):
                 for u in range(WORD_HALVES):
-                    nc.tensor.transpose(ct[:, k, u, :], c_words[:, k, u, :, 0], ident_f32[:])
+                    nc.tensor.transpose(ct[:, k, u, :], c_words[:, k, u * P : (u + 1) * P], ident_f32[:])
             c_grouped = grouped.tile([P, PAIR, SEQS, PACK], BF16, align_bytes=64)
             nc.scalar.copy(out=c_grouped[:].bitcast(F32)[:, :n], in_=ct[:, :n].rearrange("p k u j -> p k j u"))
             c_values[r] = c_grouped
@@ -196,7 +195,7 @@ def tile_infonceloss_pa_t_e_kernel(tc, embeddings, contexts, W_words, W_scales, 
                         nc.tensor.matmul_mx(
                             out=xw_bank[:, t, :],
                             lhsT=w_codes[:, X_PASSES * step + g, e_cols].bitcast(FP8X4),
-                            lhsT_scale=w_scales[:, X_PASSES * step + g, e_cols],
+                            lhsT_scale=w_scales[4 * (X_PASSES * step + g) :, e_cols],
                             rhs=x_codes[i // PAIR][:, i % PAIR, g, :].bitcast(FP8X4),
                             rhs_scale=x_scales[i // PAIR][:, i % PAIR, g, :],
                             start=(g == 0),
@@ -278,8 +277,6 @@ def tile_infonceloss_pa_t_e_kernel(tc, embeddings, contexts, W_words, W_scales, 
                 transpose_c(turn - 2)
             if live(turn - 3):
                 statistics(turn - 3)
-            if live(turn - 1):
-                pair_up_c(turn - 1)
             if live(turn):
                 transpose_x(turn)
             if live(turn - 2):
@@ -287,6 +284,8 @@ def tile_infonceloss_pa_t_e_kernel(tc, embeddings, contexts, W_words, W_scales, 
                 quantise_xw(turn - 2)
             if live(turn):
                 quantise_x(turn)
+            if turn == 1:
+                permute_w()
             if live(turn - 1):
                 first_contraction(turn - 1)
             if live(turn - 2):

@@ -29,6 +29,7 @@ WORD_HALVES = 2
 PAIR = 2
 ROUNDS = (TIMES + PAIR - 1) // PAIR
 TILES = STEPS * TIMES - 1
+HEAD_ROUNDS = 2
 
 FLOPS = 2 * TILES * SEQS * DX * DY + 2 * TILES * SEQS * SEQS * DY
 BYTES = SEQS * TIMES * (DX + DY) * 2 + STEPS * DX * DY + STEPS * DX * DY // 32 + TILES * SEQS * 4
@@ -79,10 +80,14 @@ def tile_infonceloss_pa_t_e_kernel(tc, embeddings, contexts, W_words, W_scales, 
         x_sb = {}
         c_sb = {}
 
-        def load_x(r):
+        def load_x(r, pieces=1):
             n = len(times_of(r))
             x_rows = inputs.tile([P, n, DX], BF16, name="x_rows%d" % r)
-            nc.sync.dma_start(out=x_rows[:], in_=embeddings[:, 1 + PAIR * r : 1 + PAIR * r + n, :])
+            for k in range(0, n, n // pieces):
+                some = slice(k, k + n // pieces)
+                nc.sync.dma_start(
+                    out=x_rows[:, some], in_=embeddings[:, 1 + PAIR * r + some.start : 1 + PAIR * r + some.stop, :]
+                )
             x_sb[r] = x_rows
 
         def load_c(r):
@@ -91,9 +96,8 @@ def tile_infonceloss_pa_t_e_kernel(tc, embeddings, contexts, W_words, W_scales, 
             nc.sync.dma_start(out=c_rows[:], in_=contexts[:, PAIR * r : PAIR * r + n, :])
             c_sb[r] = c_rows
 
-        load_x(0)
+        load_x(0, pieces=PAIR)
         load_x(1)
-        load_c(0)
         scale_words = W_scales.bitcast(I32)
         for quadrant in range(4):
             nc.sync.dma_start(
@@ -107,6 +111,7 @@ def tile_infonceloss_pa_t_e_kernel(tc, embeddings, contexts, W_words, W_scales, 
                 out=w_loaded[:, passes, :],
                 in_=code_words[passes].rearrange("g p n -> p g n"),
             )
+        load_c(0)
         for r in range(2, ROUNDS):
             load_x(r)
             load_c(r - 1)
@@ -137,7 +142,7 @@ def tile_infonceloss_pa_t_e_kernel(tc, embeddings, contexts, W_words, W_scales, 
             x_words = x_sb[r][:].bitcast(F32)
             x_grouped = grouped.tile([P, PAIR, X_PASSES, SEQS, PACK], BF16, align_bytes=64)
             for k in range(len(times_of(r))):
-                xt = xt_banks.tile([P, X_PASSES, WORD_HALVES, SEQS], F32)
+                xt = xt_banks.tile([P, X_PASSES, WORD_HALVES, SEQS], F32, name="xt")
                 for g in range(X_PASSES):
                     for u in range(WORD_HALVES):
                         first = g * K_PASS // 2 + u
@@ -146,15 +151,18 @@ def tile_infonceloss_pa_t_e_kernel(tc, embeddings, contexts, W_words, W_scales, 
                             x_words[:, k, first : (g + 1) * K_PASS // 2 : WORD_HALVES],
                             ident_f32[:],
                         )
-                nc.vector.tensor_copy(
-                    out=x_grouped[:].bitcast(F32)[:, k], in_=xt[:].rearrange("p g u b -> p g b u")
-                )
+                by_scalar = r < HEAD_ROUNDS or (r % 2 == 1 and k == 1)
+                empty_bank = nc.scalar.copy if by_scalar else nc.vector.tensor_copy
+                empty_bank(out=x_grouped[:].bitcast(F32)[:, k], in_=xt[:].rearrange("p g u b -> p g b u"))
             x_values[r] = x_grouped
 
         def transpose_c(r):
             n = len(times_of(r))
             c_words = c_sb[r][:].bitcast(F32)
-            ct = ct_banks.tile([P, PAIR, WORD_HALVES, SEQS], F32)
+            if r == ROUNDS - 1:
+                ct = xt_banks.tile([P, PAIR, WORD_HALVES, SEQS], F32, name="xt")
+            else:
+                ct = ct_banks.tile([P, PAIR, WORD_HALVES, SEQS], F32, name="ct")
             for k in range(n):
                 for u in range(WORD_HALVES):
                     nc.tensor.transpose(ct[:, k, u, :], c_words[:, k, u * P : (u + 1) * P], ident_f32[:])
@@ -219,7 +227,10 @@ def tile_infonceloss_pa_t_e_kernel(tc, embeddings, contexts, W_words, W_scales, 
             xw_codes[r], xw_scales[r] = wq, ws
 
         def second_contraction(r):
-            score_bank = score_banks.tile([P, PAIR * STEPS, SEQS], F32)
+            if r == ROUNDS - 1:
+                score_bank = xt_banks.tile([P, PAIR * STEPS, SEQS], F32, name="xt")
+            else:
+                score_bank = score_banks.tile([P, PAIR * STEPS, SEQS], F32, name="score_bank")
             for m, (s, step) in enumerate(pair_tiles_of(r)):
                 nc.tensor.matmul_mx(
                     out=score_bank[:, m, :],
@@ -236,9 +247,18 @@ def tile_infonceloss_pa_t_e_kernel(tc, embeddings, contexts, W_words, W_scales, 
             s, step = pair_tiles_of(r)[0]
             return column_of(s, step)
 
-        def statistics(r):
+        def row_maxima(r):
             n = len(pair_tiles_of(r))
-            for m in range(n):
+            nc.vector.tensor_reduce(
+                out=neg_max[:, first_column(r) : first_column(r) + n],
+                in_=scores[r][:, :n],
+                axis=AXIS.X,
+                op=ALU.max,
+                negate=True,
+            )
+
+        def diagonals(r):
+            for m in range(len(pair_tiles_of(r))):
                 column = slice(first_column(r) + m, first_column(r) + m + 1)
                 on_diagonal = work.tile([P, SEQS], F32)
                 nc.vector.scalar_tensor_tensor(
@@ -250,14 +270,9 @@ def tile_infonceloss_pa_t_e_kernel(tc, embeddings, contexts, W_words, W_scales, 
                     op1=ALU.mult,
                     accum_out=diagonal[:, column],
                 )
-            nc.vector.tensor_reduce(
-                out=neg_max[:, first_column(r) : first_column(r) + n],
-                in_=scores[r][:, :n],
-                axis=AXIS.X,
-                op=ALU.max,
-                negate=True,
-            )
-            for m in range(n):
+
+        def exponentials(r):
+            for m in range(len(pair_tiles_of(r))):
                 column = slice(first_column(r) + m, first_column(r) + m + 1)
                 exp_values = work.tile([P, SEQS], F32)
                 nc.scalar.activation(
@@ -272,24 +287,32 @@ def tile_infonceloss_pa_t_e_kernel(tc, embeddings, contexts, W_words, W_scales, 
         def live(r):
             return 0 <= r < ROUNDS
 
-        for turn in range(ROUNDS + 3):
-            if live(turn - 2):
+        for turn in range(ROUNDS + 2):
+            if live(turn - 2) and turn - 2 < ROUNDS - 1:
                 transpose_c(turn - 2)
-            if live(turn - 3):
-                statistics(turn - 3)
+            if turn == ROUNDS:
+                transpose_c(ROUNDS - 1)
+            if live(turn - 3) and turn - 3 < ROUNDS - 2:
+                row_maxima(turn - 3)
+                diagonals(turn - 3)
+                exponentials(turn - 3)
+            if live(turn - 2):
+                quantise_xw(turn - 2)
+                quantise_c(turn - 2)
             if live(turn):
                 transpose_x(turn)
-            if live(turn - 2):
-                quantise_c(turn - 2)
-                quantise_xw(turn - 2)
-            if live(turn):
                 quantise_x(turn)
-            if turn == 1:
+            if turn == 0:
                 permute_w()
             if live(turn - 1):
                 first_contraction(turn - 1)
             if live(turn - 2):
                 second_contraction(turn - 2)
+        for r in (ROUNDS - 2, ROUNDS - 1):
+            row_maxima(r)
+            exponentials(r)
+        for r in (ROUNDS - 2, ROUNDS - 1):
+            diagonals(r)
 
         shift = consts.tile([P, TILES], F32)
         nc.vector.tensor_tensor(out=shift[:], in0=neg_max[:], in1=diagonal[:], op=ALU.add)

@@ -43,6 +43,10 @@ def pair_tiles_of(r):
     return [(i - step, step) for i in times_of(r) for step in reversed(range(STEPS)) if i - step >= 0]
 
 
+def lined_up_times(r):
+    return [0] if HEAD_ROUNDS <= r else []
+
+
 def column_of(s, step):
     return STEPS * s + step
 
@@ -57,6 +61,7 @@ def tile_infonceloss_pa_t_e_kernel(tc, embeddings, contexts, W_words, W_scales, 
         c_mx = ctx.enter_context(tc.tile_pool(name="c_mx", bufs=3))
         xw_mx = ctx.enter_context(tc.tile_pool(name="xw_mx", bufs=2))
         work = ctx.enter_context(tc.tile_pool(name="work", bufs=2))
+        lined = ctx.enter_context(tc.tile_pool(name="lined", bufs=2))
         xt_banks = ctx.enter_context(tc.psum_pool(name="xt_banks", bufs=PAIR))
         ct_banks = ctx.enter_context(tc.psum_pool(name="ct_banks", bufs=1))
         xw_banks = ctx.enter_context(tc.psum_pool(name="xw_banks", bufs=PAIR * STEPS))
@@ -137,6 +142,17 @@ def tile_infonceloss_pa_t_e_kernel(tc, embeddings, contexts, W_words, W_scales, 
         x_values, c_values, xw_values = {}, {}, {}
         xw_codes, xw_scales = {}, {}
         scores = {}
+        x_lines = {}
+
+        def line_up_x(r):
+            x_words = x_sb[r][:].bitcast(I32)
+            for k in lined_up_times(r):
+                x_lined = lined.tile([P, X_PASSES, WORD_HALVES, P], I32)
+                nc.vector.tensor_copy(
+                    out=x_lined[:],
+                    in_=x_words[:, k, :].rearrange("b (g p u) -> b g u p", g=X_PASSES, u=WORD_HALVES),
+                )
+                x_lines[(r, k)] = x_lined
 
         def transpose_x(r):
             x_words = x_sb[r][:].bitcast(F32)
@@ -146,11 +162,11 @@ def tile_infonceloss_pa_t_e_kernel(tc, embeddings, contexts, W_words, W_scales, 
                 for g in range(X_PASSES):
                     for u in range(WORD_HALVES):
                         first = g * K_PASS // 2 + u
-                        nc.tensor.transpose(
-                            xt[:, g, u, :],
-                            x_words[:, k, first : (g + 1) * K_PASS // 2 : WORD_HALVES],
-                            ident_f32[:],
-                        )
+                        if (r, k) in x_lines:
+                            words = x_lines[(r, k)][:, g, u, :].bitcast(F32)
+                        else:
+                            words = x_words[:, k, first : (g + 1) * K_PASS // 2 : WORD_HALVES]
+                        nc.tensor.transpose(xt[:, g, u, :], words, ident_f32[:])
                 by_scalar = r < HEAD_ROUNDS or (r % 2 == 1 and k == 1)
                 empty_bank = nc.scalar.copy if by_scalar else nc.vector.tensor_copy
                 empty_bank(out=x_grouped[:].bitcast(F32)[:, k], in_=xt[:].rearrange("p g u b -> p g b u"))
@@ -301,6 +317,9 @@ def tile_infonceloss_pa_t_e_kernel(tc, embeddings, contexts, W_words, W_scales, 
                 quantise_c(turn - 2)
             if live(turn):
                 transpose_x(turn)
+            if live(turn + 1):
+                line_up_x(turn + 1)
+            if live(turn):
                 quantise_x(turn)
             if turn == 0:
                 permute_w()
@@ -318,16 +337,19 @@ def tile_infonceloss_pa_t_e_kernel(tc, embeddings, contexts, W_words, W_scales, 
         nc.vector.tensor_tensor(out=shift[:], in0=neg_max[:], in1=diagonal[:], op=ALU.add)
         log_sum = consts.tile([P, TILES], F32)
         nc.scalar.activation(out=log_sum[:], in_=sum_exp[:], func=ACT.Ln)
-        centred = consts.tile([P, TILES], F32)
-        nc.vector.tensor_tensor(out=centred[:], in0=log_sum[:], in1=shift[:], op=ALU.subtract)
         first_row = 0
-        for step in range(STEPS):
+        for step, queue in zip(range(STEPS), (nc.sync, nc.scalar)):
             n_times = TIMES - step
             loss = consts.tile([P, n_times], F32, name="loss%d" % step)
-            nc.vector.tensor_scalar_add(
-                out=loss[:], in0=centred[:, step:TILES:STEPS], scalar1=-math.log(SEQS * n_times)
+            nc.vector.scalar_tensor_tensor(
+                out=loss[:],
+                in0=log_sum[:, step:TILES:STEPS],
+                scalar=-math.log(SEQS * n_times),
+                in1=shift[:, step:TILES:STEPS],
+                op0=ALU.add,
+                op1=ALU.subtract,
             )
-            nc.sync.dma_start(
+            queue.dma_start(
                 out=out[first_row : first_row + SEQS * n_times].rearrange("(b s) -> b s", s=n_times),
                 in_=loss[:],
             )

@@ -143,6 +143,7 @@ def tile_infonceloss_pa_t_e_kernel(tc, embeddings, contexts, W_words, W_scales, 
         xw_codes, xw_scales = {}, {}
         scores = {}
         x_lines = {}
+        x_banks = {}
 
         def line_up_x(r):
             x_words = x_sb[r][:].bitcast(I32)
@@ -157,8 +158,10 @@ def tile_infonceloss_pa_t_e_kernel(tc, embeddings, contexts, W_words, W_scales, 
         def transpose_x(r):
             x_words = x_sb[r][:].bitcast(F32)
             x_grouped = grouped.tile([P, PAIR, X_PASSES, SEQS, PACK], BF16, align_bytes=64)
+            x_values[r] = x_grouped
             for k in range(len(times_of(r))):
                 xt = xt_banks.tile([P, X_PASSES, WORD_HALVES, SEQS], F32, name="xt")
+                x_banks[(r, k)] = xt
                 for g in range(X_PASSES):
                     for u in range(WORD_HALVES):
                         first = g * K_PASS // 2 + u
@@ -167,10 +170,15 @@ def tile_infonceloss_pa_t_e_kernel(tc, embeddings, contexts, W_words, W_scales, 
                         else:
                             words = x_words[:, k, first : (g + 1) * K_PASS // 2 : WORD_HALVES]
                         nc.tensor.transpose(xt[:, g, u, :], words, ident_f32[:])
+
+        def empty_x_banks(r, scalars_share):
+            for k in range(len(times_of(r))):
                 by_scalar = r < HEAD_ROUNDS or (r % 2 == 1 and k == 1)
-                empty_bank = nc.scalar.copy if by_scalar else nc.vector.tensor_copy
-                empty_bank(out=x_grouped[:].bitcast(F32)[:, k], in_=xt[:].rearrange("p g u b -> p g b u"))
-            x_values[r] = x_grouped
+                if by_scalar == scalars_share:
+                    empty_bank = nc.scalar.copy if by_scalar else nc.vector.tensor_copy
+                    empty_bank(
+                        out=x_values[r][:].bitcast(F32)[:, k], in_=x_banks[(r, k)][:].rearrange("p g u b -> p g b u")
+                    )
 
         def transpose_c(r):
             n = len(times_of(r))
@@ -245,6 +253,8 @@ def tile_infonceloss_pa_t_e_kernel(tc, embeddings, contexts, W_words, W_scales, 
         def second_contraction(r):
             if r == ROUNDS - 1:
                 score_bank = xt_banks.tile([P, PAIR * STEPS, SEQS], F32, name="xt")
+            elif r == ROUNDS - 2:
+                score_bank = xw_banks.tile([P, PAIR * STEPS, SEQS], F32, name="xw_bank")
             else:
                 score_bank = score_banks.tile([P, PAIR * STEPS, SEQS], F32, name="score_bank")
             for m, (s, step) in enumerate(pair_tiles_of(r)):
@@ -303,31 +313,39 @@ def tile_infonceloss_pa_t_e_kernel(tc, embeddings, contexts, W_words, W_scales, 
         def live(r):
             return 0 <= r < ROUNDS
 
-        for turn in range(ROUNDS + 2):
-            if live(turn - 2) and turn - 2 < ROUNDS - 1:
+        for turn in range(ROUNDS):
+            if live(turn - 2):
                 transpose_c(turn - 2)
-            if turn == ROUNDS:
-                transpose_c(ROUNDS - 1)
-            if live(turn - 3) and turn - 3 < ROUNDS - 2:
+            transpose_x(turn)
+            empty_x_banks(turn, scalars_share=True)
+            if live(turn - 3):
                 row_maxima(turn - 3)
                 diagonals(turn - 3)
                 exponentials(turn - 3)
             if live(turn - 2):
                 quantise_xw(turn - 2)
                 quantise_c(turn - 2)
-            if live(turn):
-                transpose_x(turn)
+            empty_x_banks(turn, scalars_share=False)
             if live(turn + 1):
                 line_up_x(turn + 1)
-            if live(turn):
-                quantise_x(turn)
+            quantise_x(turn)
             if turn == 0:
                 permute_w()
             if live(turn - 1):
                 first_contraction(turn - 1)
             if live(turn - 2):
                 second_contraction(turn - 2)
+
+        transpose_c(ROUNDS - 2)
+        transpose_c(ROUNDS - 1)
+        first_contraction(ROUNDS - 1)
+        row_maxima(ROUNDS - 3)
+        diagonals(ROUNDS - 3)
+        exponentials(ROUNDS - 3)
         for r in (ROUNDS - 2, ROUNDS - 1):
+            quantise_xw(r)
+            quantise_c(r)
+            second_contraction(r)
             row_maxima(r)
             exponentials(r)
         for r in (ROUNDS - 2, ROUNDS - 1):

import math
from contextlib import ExitStack

import concourse.mybir as mybir
from concourse.masks import make_identity

F32 = mybir.dt.float32
BF16 = mybir.dt.bfloat16
I32 = mybir.dt.int32
U32 = mybir.dt.uint32
U8 = mybir.dt.uint8
FP8X4 = mybir.dt.float8_e4m3fn_x4
ALU = mybir.AluOpType
ACT = mybir.ActivationFunctionType
AXIS = mybir.AxisListType

P = 128
SEQS = 128
TIMES = 33
DX = 1024
DY = 512
STEPS = 2
PACK = 4
K_PASS = P * PACK
X_PASSES = DX // K_PASS
W_PASSES = STEPS * X_PASSES
E_CHUNKS = DY // P
WORD_HALVES = 2
PAIR = 2
ROUNDS = (TIMES + PAIR - 1) // PAIR
TILES = STEPS * TIMES - 1
HEAD_ROUNDS = 2

FLOPS = 2 * TILES * SEQS * DX * DY + 2 * TILES * SEQS * SEQS * DY
BYTES = SEQS * TIMES * (DX + DY) * 2 + STEPS * DX * DY + STEPS * DX * DY // 32 + TILES * SEQS * 4


def times_of(r):
    return list(range(PAIR * r, min(PAIR * r + PAIR, TIMES)))


def pair_tiles_of(r):
    return [(i - step, step) for i in times_of(r) for step in reversed(range(STEPS)) if i - step >= 0]


def lined_up_times(r):
    return [0] if HEAD_ROUNDS <= r else []


def column_of(s, step):
    return STEPS * s + step


def tile_infonceloss_pa_t_e_kernel(tc, embeddings, contexts, W_words, W_scales, out):
    nc = tc.nc
    with ExitStack() as ctx:
        consts = ctx.enter_context(tc.tile_pool(name="consts", bufs=1))
        inputs = ctx.enter_context(tc.tile_pool(name="inputs", bufs=1))
        grouped = ctx.enter_context(tc.tile_pool(name="grouped", bufs=2))
        x_mx = ctx.enter_context(tc.tile_pool(name="x_mx", bufs=2))
        c_mx = ctx.enter_context(tc.tile_pool(name="c_mx", bufs=3))
        xw_mx = ctx.enter_context(tc.tile_pool(name="xw_mx", bufs=2))
        work = ctx.enter_context(tc.tile_pool(name="work", bufs=2))
        lined = ctx.enter_context(tc.tile_pool(name="lined", bufs=2))
        xt_banks = ctx.enter_context(tc.psum_pool(name="xt_banks", bufs=PAIR))
        ct_banks = ctx.enter_context(tc.psum_pool(name="ct_banks", bufs=1))
        xw_banks = ctx.enter_context(tc.psum_pool(name="xw_banks", bufs=PAIR * STEPS))
        score_banks = ctx.enter_context(tc.psum_pool(name="score_banks", bufs=1))
        ctx.enter_context(tc.manual_schedule())

        ident_f32 = consts.tile([P, P], F32)
        make_identity(nc, ident_f32[:])

        w_loaded = consts.tile([P, W_PASSES, DY], I32)
        w_codes = consts.tile([P, W_PASSES, DY], I32, align_bytes=64)
        w_scales_loaded = consts.tile([P, DY], U8)
        w_scales = consts.tile([P, DY], U8, align_bytes=64)
        nc.vector.memset(w_scales_loaded[:].bitcast(I32), 0)

        zero = consts.tile([P, 1], F32)
        nc.vector.memset(zero[:], 0.0)
        one = consts.tile([P, 1], F32)
        nc.scalar.activation(out=one[:], in_=zero[:], func=ACT.Exp)

        x_sb = {}
        c_sb = {}

        def load_x(r, pieces=1):
            n = len(times_of(r))
            x_rows = inputs.tile([P, n, DX], BF16, name="x_rows%d" % r)
            for k in range(0, n, n // pieces):
                some = slice(k, k + n // pieces)
                nc.sync.dma_start(
                    out=x_rows[:, some], in_=embeddings[:, 1 + PAIR * r + some.start : 1 + PAIR * r + some.stop, :]
                )
            x_sb[r] = x_rows

        def load_c(r):
            n = len(times_of(r))
            c_rows = inputs.tile([P, n, DY], BF16, name="c_rows%d" % r)
            nc.sync.dma_start(out=c_rows[:], in_=contexts[:, PAIR * r : PAIR * r + n, :])
            c_sb[r] = c_rows

        load_x(0, pieces=PAIR)
        load_x(1)
        scale_words = W_scales.bitcast(I32)
        for quadrant in range(4):
            nc.sync.dma_start(
                out=w_scales_loaded[32 * quadrant : 32 * quadrant + 4 * W_PASSES].bitcast(I32),
                in_=scale_words[:, 4 * quadrant : 4 * quadrant + 4, :],
            )
        code_words = W_words.rearrange("g p n t -> g p (n t)").bitcast(I32)
        for step in range(STEPS):
            passes = slice(X_PASSES * step, X_PASSES * (step + 1))
            nc.sync.dma_start(
                out=w_loaded[:, passes, :],
                in_=code_words[passes].rearrange("g p n -> p g n"),
            )
        load_c(0)
        for r in range(2, ROUNDS):
            load_x(r)
            load_c(r - 1)
        load_c(ROUNDS - 1)

        def permute_w():
            nc.vector.tensor_copy(
                out=w_scales[:].rearrange("p (u h m) -> p u m h", u=WORD_HALVES, h=2),
                in_=w_scales_loaded[:].rearrange("p (u m h) -> p u m h", u=WORD_HALVES, h=2),
            )
            for g in range(W_PASSES):
                nc.vector.tensor_copy(
                    out=w_codes[:, g, :].rearrange("p (u h m) -> p u h m", u=WORD_HALVES, h=2),
                    in_=w_loaded[:, g, :].rearrange("p (u m h) -> p u h m", u=WORD_HALVES, h=2),
                )

        neg_max = consts.tile([P, TILES], F32)
        sum_exp = consts.tile([P, TILES], F32)
        diagonal = consts.tile([P, TILES], F32)

        x_codes, x_scales = {}, {}
        c_codes, c_scales = {}, {}
        x_values, c_values, xw_values = {}, {}, {}
        xw_codes, xw_scales = {}, {}
        scores = {}
        x_lines = {}
        x_banks = {}

        def line_up_x(r):
            x_words = x_sb[r][:].bitcast(I32)
            for k in lined_up_times(r):
                x_lined = lined.tile([P, X_PASSES, WORD_HALVES, P], I32)
                nc.vector.tensor_copy(
                    out=x_lined[:],
                    in_=x_words[:, k, :].rearrange("b (g p u) -> b g u p", g=X_PASSES, u=WORD_HALVES),
                )
                x_lines[(r, k)] = x_lined

        def transpose_x(r):
            x_words = x_sb[r][:].bitcast(F32)
            x_grouped = grouped.tile([P, PAIR, X_PASSES, SEQS, PACK], BF16, align_bytes=64)
            x_values[r] = x_grouped
            for k in range(len(times_of(r))):
                xt = xt_banks.tile([P, X_PASSES, WORD_HALVES, SEQS], F32, name="xt")
                x_banks[(r, k)] = xt
                for g in range(X_PASSES):
                    for u in range(WORD_HALVES):
                        first = g * K_PASS // 2 + u
                        if (r, k) in x_lines:
                            words = x_lines[(r, k)][:, g, u, :].bitcast(F32)
                        else:
                            words = x_words[:, k, first : (g + 1) * K_PASS // 2 : WORD_HALVES]
                        nc.tensor.transpose(xt[:, g, u, :], words, ident_f32[:])

        def empty_x_banks(r, scalars_share):
            for k in range(len(times_of(r))):
                by_scalar = r < HEAD_ROUNDS or (r % 2 == 1 and k == 1)
                if by_scalar == scalars_share:
                    empty_bank = nc.scalar.copy if by_scalar else nc.vector.tensor_copy
                    empty_bank(
                        out=x_values[r][:].bitcast(F32)[:, k], in_=x_banks[(r, k)][:].rearrange("p g u b -> p g b u")
                    )

        def transpose_c(r):
            n = len(times_of(r))
            c_words = c_sb[r][:].bitcast(F32)
            if r == ROUNDS - 1:
                ct = xt_banks.tile([P, PAIR, WORD_HALVES, SEQS], F32, name="xt")
            else:
                ct = ct_banks.tile([P, PAIR, WORD_HALVES, SEQS], F32, name="ct")
            for k in range(n):
                for u in range(WORD_HALVES):
                    nc.tensor.transpose(ct[:, k, u, :], c_words[:, k, u * P : (u + 1) * P], ident_f32[:])
            c_grouped = grouped.tile([P, PAIR, SEQS, PACK], BF16, align_bytes=64)
            nc.scalar.copy(out=c_grouped[:].bitcast(F32)[:, :n], in_=ct[:, :n].rearrange("p k u j -> p k j u"))
            c_values[r] = c_grouped

        def quantise_x(r):
            n = len(times_of(r))
            xq = x_mx.tile([P, PAIR, X_PASSES, SEQS], U32, align_bytes=64)
            xs = x_mx.tile([P, PAIR, X_PASSES, SEQS], U8, align_bytes=64)
            nc.vector.quantize_mx(
                out=xq[:, :n].rearrange("p k g b -> p (k g b)").bitcast(FP8X4),
                scales=xs[:, :n].rearrange("p k g b -> p (k g b)"),
                in_=x_values[r][:, :n].rearrange("p k g b t -> p (k g b t)"),
            )
            x_codes[r], x_scales[r] = xq, xs

        def quantise_c(r):
            n = len(times_of(r))
            cq = c_mx.tile([P, PAIR, SEQS], U32, align_bytes=64)
            cs = c_mx.tile([P, PAIR, SEQS], U8, align_bytes=64)
            nc.vector.quantize_mx(
                out=cq[:, :n].rearrange("p k j -> p (k j)").bitcast(FP8X4),
                scales=cs[:, :n].rearrange("p k j -> p (k j)"),
                in_=c_values[r][:, :n].rearrange("p k j t -> p (k j t)"),
            )
            c_codes[r], c_scales[r] = cq, cs

        def first_contraction(r):
            xw_grouped = grouped.tile([P, PAIR * STEPS, SEQS, PACK], BF16, align_bytes=64)
            for m, (s, step) in enumerate(pair_tiles_of(r)):
                i = s + step
                xw_bank = xw_banks.tile([P, E_CHUNKS, SEQS], F32)
                for t in range(E_CHUNKS):
                    e_cols = slice(t * P, (t + 1) * P)
                    for g in range(X_PASSES):
                        nc.tensor.matmul_mx(
                            out=xw_bank[:, t, :],
                            lhsT=w_codes[:, X_PASSES * step + g, e_cols].bitcast(FP8X4),
                            lhsT_scale=w_scales[4 * (X_PASSES * step + g) :, e_cols],
                            rhs=x_codes[i // PAIR][:, i % PAIR, g, :].bitcast(FP8X4),
                            rhs_scale=x_scales[i // PAIR][:, i % PAIR, g, :],
                            start=(g == 0),
                            stop=(g == X_PASSES - 1),
                        )
                nc.scalar.copy(out=xw_grouped[:, m], in_=xw_bank[:].rearrange("p t b -> p b t"))
            xw_values[r] = xw_grouped

        def quantise_xw(r):
            wq = xw_mx.tile([P, PAIR * STEPS, SEQS], U32, align_bytes=64)
            ws = xw_mx.tile([P, PAIR * STEPS, SEQS], U8, align_bytes=64)
            tiles = pair_tiles_of(r)
            for i in times_of(r):
                mine = [m for m, (s, step) in enumerate(tiles) if s + step == i]
                slots = slice(mine[0], mine[-1] + 1)
                nc.vector.quantize_mx(
                    out=wq[:, slots].rearrange("p m b -> p (m b)").bitcast(FP8X4),
                    scales=ws[:, slots].rearrange("p m b -> p (m b)"),
                    in_=xw_values[r][:, slots].rearrange("p m b t -> p (m b t)"),
                )
            xw_codes[r], xw_scales[r] = wq, ws

        def second_contraction(r):
            if r == ROUNDS - 1:
                score_bank = xt_banks.tile([P, PAIR * STEPS, SEQS], F32, name="xt")
            elif r == ROUNDS - 2:
                score_bank = xw_banks.tile([P, PAIR * STEPS, SEQS], F32, name="xw_bank")
            else:
                score_bank = score_banks.tile([P, PAIR * STEPS, SEQS], F32, name="score_bank")
            for m, (s, step) in enumerate(pair_tiles_of(r)):
                nc.tensor.matmul_mx(
                    out=score_bank[:, m, :],
                    lhsT=xw_codes[r][:, m, :].bitcast(FP8X4),
                    lhsT_scale=xw_scales[r][:, m, :],
                    rhs=c_codes[s // PAIR][:, s % PAIR, :].bitcast(FP8X4),
                    rhs_scale=c_scales[s // PAIR][:, s % PAIR, :],
                    start=True,
                    stop=True,
                )
            scores[r] = score_bank

        def first_column(r):
            s, step = pair_tiles_of(r)[0]
            return column_of(s, step)

        def row_maxima(r):
            n = len(pair_tiles_of(r))
            nc.vector.tensor_reduce(
                out=neg_max[:, first_column(r) : first_column(r) + n],
                in_=scores[r][:, :n],
                axis=AXIS.X,
                op=ALU.max,
                negate=True,
            )

        def diagonals(r):
            for m in range(len(pair_tiles_of(r))):
                column = slice(first_column(r) + m, first_column(r) + m + 1)
                on_diagonal = work.tile([P, SEQS], F32)
                nc.vector.scalar_tensor_tensor(
                    out=on_diagonal[:],
                    in0=scores[r][:, m, :],
                    scalar=1.0,
                    in1=ident_f32[:],
                    op0=ALU.mult,
                    op1=ALU.mult,
                    accum_out=diagonal[:, column],
                )

        def exponentials(r):
            for m in range(len(pair_tiles_of(r))):
                column = slice(first_column(r) + m, first_column(r) + m + 1)
                exp_values = work.tile([P, SEQS], F32)
                nc.scalar.activation(
                    out=exp_values[:],
                    in_=scores[r][:, m, :],
                    func=ACT.Exp,
                    bias=neg_max[:, column],
                    scale=1.0,
                    accum_out=sum_exp[:, column],
                )

        def live(r):
            return 0 <= r < ROUNDS

        for turn in range(ROUNDS):
            if live(turn - 2):
                transpose_c(turn - 2)
            transpose_x(turn)
            empty_x_banks(turn, scalars_share=True)
            if live(turn - 3):
                row_maxima(turn - 3)
                diagonals(turn - 3)
                exponentials(turn - 3)
            if live(turn - 2):
                quantise_xw(turn - 2)
                quantise_c(turn - 2)
            empty_x_banks(turn, scalars_share=False)
            if live(turn + 1):
                line_up_x(turn + 1)
            quantise_x(turn)
            if turn == 0:
                permute_w()
            if live(turn - 1):
                first_contraction(turn - 1)
            if live(turn - 2):
                second_contraction(turn - 2)

        transpose_c(ROUNDS - 2)
        transpose_c(ROUNDS - 1)
        first_contraction(ROUNDS - 1)
        row_maxima(ROUNDS - 3)
        diagonals(ROUNDS - 3)
        exponentials(ROUNDS - 3)
        for r in (ROUNDS - 2, ROUNDS - 1):
            quantise_xw(r)
            quantise_c(r)
            second_contraction(r)
            row_maxima(r)
            exponentials(r)
        for r in (ROUNDS - 2, ROUNDS - 1):
            diagonals(r)

        shift = consts.tile([P, TILES], F32)
        nc.vector.tensor_tensor(out=shift[:], in0=neg_max[:], in1=diagonal[:], op=ALU.add)
        log_sum = consts.tile([P, TILES], F32)
        nc.scalar.activation(out=log_sum[:], in_=sum_exp[:], func=ACT.Ln)
        first_row = 0
        for step, queue in zip(range(STEPS), (nc.sync, nc.scalar)):
            n_times = TIMES - step
            loss = consts.tile([P, n_times], F32, name="loss%d" % step)
            nc.vector.scalar_tensor_tensor(
                out=loss[:],
                in0=log_sum[:, step:TILES:STEPS],
                scalar=-math.log(SEQS * n_times),
                in1=shift[:, step:TILES:STEPS],
                op0=ALU.add,
                op1=ALU.subtract,
            )
            queue.dma_start(
                out=out[first_row : first_row + SEQS * n_times].rearrange("(b s) -> b s", s=n_times),
                in_=loss[:],
            )
            first_row += SEQS * n_times
